import numpy as np
import ml_dtypes


def mxq(x, axis, fmt="e4m3"):
    dtype, down = {"e4m3": (ml_dtypes.float8_e4m3fn, 7), "e5m2": (ml_dtypes.float8_e5m2, 14)}[fmt]
    v = np.moveaxis(np.asarray(x, np.float32).astype(ml_dtypes.bfloat16).astype(np.float64), axis, -1)
    blocks = v.reshape(v.shape[:-1] + (-1, 32))
    amax = np.abs(blocks).max(-1, keepdims=True)
    byte = np.maximum(np.where(amax > 0, np.frexp(amax)[1] - 1 + 127, 0) - down, 1)
    scale = np.exp2(byte - 127.0)
    codes = (blocks / scale).astype(np.float32).astype(dtype).astype(np.float64)
    return np.moveaxis((codes * scale).reshape(v.shape), -1, axis)


WIDE = False


def mx_kscale(k):
    if not WIDE:
        return np.ones(k)
    levels = np.array([10, -10, 5, -5, 0])
    a = np.random.permutation(np.resize(levels, k // 512 * 4)).reshape(k // 512, 4)
    idx = np.arange(k)
    return np.exp2(a[idx // 512, idx % 128 // 32])


BF16 = ml_dtypes.bfloat16


def bf(x):
    return np.asarray(x, np.float32).astype(BF16)


def f64(x):
    return np.asarray(x).astype(np.float64)


E, T, H, D, R = 4, 256, 1024, 1024, 128
SCALE = 2.0


def setup_inputs():
    s = mx_kscale(D)
    return {"h": bf(np.random.standard_normal((E, T, D)) * 0.8 * s),
            "low_d": bf(np.random.standard_normal((E, T, R)) * 1.2),
            "W_d": bf(np.random.standard_normal((E, H, D)) * 1.5 / np.sqrt(D) / s),
            "B_d": bf(np.random.standard_normal((E, H, R)) * 0.3 / np.sqrt(R))}


def reference(h, low_d, W_d, B_d):
    base = mxq(f64(h), 2, "e4m3") @ mxq(f64(W_d), 2, "e4m3").transpose(0, 2, 1)
    delta = f64(low_d) @ f64(B_d).transpose(0, 2, 1)
    out = base + SCALE * delta
    return out.reshape(-1, H)

@@ -1,0 +1,205 @@
+from contextlib import ExitStack
+
+import concourse.mybir as mybir
+from concourse.masks import make_identity
+
+F32 = mybir.dt.float32
+BF16 = mybir.dt.bfloat16
+U32 = mybir.dt.uint32
+U8 = mybir.dt.uint8
+FP8X4 = mybir.dt.float8_e4m3fn_x4
+MULT = mybir.AluOpType.mult
+ADD = mybir.AluOpType.add
+
+P = 128
+E, T, H, D, R = 4, 256, 1024, 1024, 128
+SCALE = 2.0
+FLOPS = 2 * E * T * H * (D + R)
+NCHUNK = 2 * E
+
+
+def tile_loralinearexpertswrapper_pb_kernel(tc, h, low_d, W_d, B_d, out):
+    nc = tc.nc
+    with ExitStack() as ctx:
+        keep = ctx.enter_context(tc.tile_pool(name="keep", bufs=1))
+        grp_pool = ctx.enter_context(tc.tile_pool(name="grp", bufs=3))
+        hgrp_pool = ctx.enter_context(tc.tile_pool(name="hgrp", bufs=2))
+        wq_pool = ctx.enter_context(tc.tile_pool(name="wq", bufs=3))
+        tp = ctx.enter_context(tc.psum_pool(name="tp", bufs=4))
+        accp = ctx.enter_context(tc.psum_pool(name="accp", bufs=4))
+        ctx.enter_context(tc.manual_schedule())
+
+        ident_bf = keep.tile([P, P], BF16, name="ident_bf")
+        make_identity(nc, ident_bf[:])
+        ident_f = keep.tile([P, P], F32, name="ident_f")
+        make_identity(nc, ident_f[:])
+
+        low_sb = keep.tile([P, E, 2 * R], BF16, name="low_sb")
+        nc.sync.dma_start(out=low_sb[:], in_=low_d.rearrange("e (p i) r -> p e (i r)", i=2))
+        b_sb = []
+        for e in range(E):
+            b_t = keep.tile([P, 2, 4 * R], BF16, name="b_sb%d" % e)
+            nc.sync.dma_start(out=b_t[:], in_=B_d[e].rearrange("(c p i) r -> p c (i r)", c=2, i=4))
+            b_sb.append(b_t)
+        h_sb = []
+        w_sb = []
+        for e in range(E):
+            h_t = keep.tile([P, 2 * D], BF16, name="h_sb%d" % e)
+            nc.sync.dma_start(out=h_t[:], in_=h[e].rearrange("(p i) k -> p (i k)", i=2))
+            h_sb.append(h_t)
+            for c in range(2):
+                w_t = keep.tile([P, 4 * D], BF16, name="w_sb%d" % (2 * e + c))
+                nc.sync.dma_start(
+                    out=w_t[:],
+                    in_=W_d[e, 512 * c : 512 * c + 512, :].rearrange("(p i) k -> p (i k)", i=4),
+                )
+                w_sb.append(w_t)
+
+        low_t = keep.tile([P, 2 * E, P], BF16, name="low_t")
+        b_tr = [keep.tile([P, 2, 512], BF16, name="b_tr%d" % e) for e in range(E)]
+        o_sb = [keep.tile([P, 2, H], F32, name="o_sb%d" % e) for e in range(E)]
+        h_codes = [keep.tile([P, 2, T], U32, name="h_codes%d" % e, align_bytes=64) for e in range(E)]
+        h_scales = [keep.tile([P, 2, T], U8, name="h_scales%d" % e, align_bytes=64) for e in range(E)]
+
+        def copy_out(on_scalar, dst, src):
+            if on_scalar:
+                nc.scalar.copy(out=dst, in_=src)
+            else:
+                nc.vector.tensor_copy(out=dst, in_=src)
+
+        def low_transposes():
+            for half in range(2):
+                xl = tp.tile([P, 4, P], BF16, name="xl", tag="tp")
+                for s in range(4):
+                    e, i = divmod(4 * half + s, 2)
+                    nc.tensor.transpose(xl[:, s, :], low_sb[:, e, P * i : P * i + P], ident_bf[:])
+                copy_out(half == 1, low_t[:, 4 * half : 4 * half + 4, :], xl[:])
+
+        def b_transposes(e):
+            for c in range(2):
+                xb = tp.tile([P, 4, P], BF16, name="xb", tag="tp")
+                for i in range(4):
+                    nc.tensor.transpose(xb[:, i, :], b_sb[e][:, c, P * i : P * i + P], ident_bf[:])
+                copy_out(c == 1, b_tr[e][:, c, :], xb[:].rearrange("p i q -> p (i q)"))
+
+        def lora(e):
+            for c in range(2):
+                for i2 in range(2):
+                    acc = accp.tile([P, 512], F32, name="acc", tag="acc")
+                    nc.tensor.matmul(
+                        out=acc[:], lhsT=low_t[:, 2 * e + i2, :], rhs=b_tr[e][:, c, :], start=True, stop=True
+                    )
+                    copy_out(
+                        i2 == 1,
+                        o_sb[e][:, i2, 512 * c : 512 * c + 512].rearrange("p (q i) -> p q i", i=4),
+                        acc[:].rearrange("p (i q) -> p q i", i=4),
+                    )
+
+        def word_transposes(src_f32, tiles_of_bank, g, dst_f32, on_scalar):
+            xt = tp.tile([P, 2, 256], F32, name="xt", tag="tp")
+            for u in range(2):
+                for s in range(2):
+                    col = 512 * tiles_of_bank[s] + 256 * g + P * u
+                    nc.tensor.transpose(xt[:, u, P * s : P * s + P], src_f32[:, col : col + P], ident_f[:])
+            copy_out(on_scalar, dst_f32.rearrange("p (n u) -> p n u", u=2), xt[:].rearrange("p u n -> p n u"))
+
+        def h_transposes(e):
+            hg = hgrp_pool.tile([P, 8 * T], BF16, name="hg", align_bytes=64)
+            hgf = hg[:].bitcast(F32)
+            hf = h_sb[e][:].bitcast(F32)
+            for g in range(2):
+                word_transposes(hf, (0, 1), g, hgf[:, 512 * g : 512 * g + 512], True)
+            return hg
+
+        def h_quantise(e, hg):
+            nc.vector.quantize_mx(
+                out=h_codes[e][:].rearrange("p g n -> p (g n)").bitcast(FP8X4),
+                scales=h_scales[e][:].rearrange("p g n -> p (g n)"),
+                in_=hg[:],
+            )
+
+        def w_transposes(j):
+            grp = grp_pool.tile([P, 4096], BF16, name="grp", align_bytes=64)
+            gf = grp[:].bitcast(F32)
+            wf = w_sb[j][:].bitcast(F32)
+            for g in range(2):
+                for ih in range(2):
+                    lo = 1024 * g + 512 * ih
+                    word_transposes(wf, (2 * ih, 2 * ih + 1), g, gf[:, lo : lo + 512], True)
+            w_codes = wq_pool.tile([P, 2, 512], U32, name="w_codes", align_bytes=64)
+            w_scales = wq_pool.tile([P, 2, 512], U8, name="w_scales", align_bytes=64)
+            return grp, w_codes, w_scales
+
+        def w_quantise(st, g):
+            grp, w_codes, w_scales = st
+            nc.vector.quantize_mx(
+                out=w_codes[:, g, :].bitcast(FP8X4),
+                scales=w_scales[:, g, :],
+                in_=grp[:, 2048 * g : 2048 * g + 2048],
+            )
+
+        def mx_passes(j, st):
+            e = j // 2
+            w_codes, w_scales = st[1], st[2]
+            accs = [accp.tile([P, 512], F32, name="macc%d" % i2, tag="acc") for i2 in range(2)]
+            for g in range(2):
+                for i2 in range(2):
+                    nc.tensor.matmul_mx(
+                        out=accs[i2][:],
+                        lhsT=h_codes[e][:, g, P * i2 : P * i2 + P].bitcast(FP8X4),
+                        lhsT_scale=h_scales[e][:, g, P * i2 : P * i2 + P],
+                        rhs=w_codes[:, g, :].bitcast(FP8X4),
+                        rhs_scale=w_scales[:, g, :],
+                        start=(g == 0),
+                        stop=(g == 1),
+                    )
+            return accs
+
+        def final_add(j, i2, accs):
+            e, c = divmod(j, 2)
+            dst = o_sb[e][:, i2, 512 * c : 512 * c + 512].rearrange("p (q i) -> p q i", i=4)
+            nc.vector.scalar_tensor_tensor(
+                out=dst, in0=dst, scalar=SCALE, in1=accs[i2][:].rearrange("p (i q) -> p q i", i=4), op0=MULT, op1=ADD
+            )
+
+        def out_rows(e):
+            return out[T * e : T * e + T, :].rearrange("(p i) n -> p i n", i=2)
+
+        low_transposes()
+        b_transposes(0)
+        b_transposes(1)
+        lora(0)
+        b_transposes(2)
+        lora(1)
+        b_transposes(3)
+        lora(2)
+        hg = h_transposes(0)
+        lora(3)
+        h_quantise(0, hg)
+        nxt = w_transposes(0)
+        w_quantise(nxt, 0)
+        w_quantise(nxt, 1)
+
+        for j in range(NCHUNK):
+            cur = nxt
+            e, c = divmod(j, 2)
+            if j + 1 < NCHUNK:
+                if c == 1:
+                    hg = h_transposes(e + 1)
+                nxt = w_transposes(j + 1)
+                if c == 1:
+                    h_quantise(e + 1, hg)
+                w_quantise(nxt, 0)
+            accs = mx_passes(j, cur)
+            final_add(j, 0, accs)
+            if j + 1 < NCHUNK:
+                w_quantise(nxt, 1)
+            if j == NCHUNK - 1:
+                nc.sync.dma_start(out=out_rows(e)[:, 0, 512:1024], in_=o_sb[e][:, 0, 512:1024])
+            final_add(j, 1, accs)
+            if j == NCHUNK - 1:
+                nc.sync.dma_start(out=out_rows(e)[:, 1, 512:1024], in_=o_sb[e][:, 1, 512:1024])
+            elif j == NCHUNK - 2:
+                nc.sync.dma_start(out=out_rows(e)[:, :, 0:512], in_=o_sb[e][:, :, 0:512])
+            elif c == 1:
+                nc.sync.dma_start(out=out_rows(e), in_=o_sb[e][:])

@@ -29,6 +29,8 @@ def tile_loralinearexpertswrapper_pb_kernel(tc, h, low_d, W_d, B_d, out):
         accp = ctx.enter_context(tc.psum_pool(name="accp", bufs=4))
         ctx.enter_context(tc.manual_schedule())
 
+        zero = keep.tile([P, 512], BF16, name="zero")
+        nc.vector.memset(zero[:], 0.0)
         ident_bf = keep.tile([P, P], BF16, name="ident_bf")
         make_identity(nc, ident_bf[:])
         ident_f = keep.tile([P, P], F32, name="ident_f")
@@ -43,17 +45,23 @@ def tile_loralinearexpertswrapper_pb_kernel(tc, h, low_d, W_d, B_d, out):
             b_sb.append(b_t)
         h_sb = []
         w_sb = []
-        for e in range(E):
+
+        def load_h(e):
             h_t = keep.tile([P, 2 * D], BF16, name="h_sb%d" % e)
             nc.sync.dma_start(out=h_t[:], in_=h[e].rearrange("(p i) k -> p (i k)", i=2))
             h_sb.append(h_t)
-            for c in range(2):
-                w_t = keep.tile([P, 4 * D], BF16, name="w_sb%d" % (2 * e + c))
-                nc.sync.dma_start(
-                    out=w_t[:],
-                    in_=W_d[e, 512 * c : 512 * c + 512, :].rearrange("(p i) k -> p (i k)", i=4),
-                )
-                w_sb.append(w_t)
+
+        load_h(0)
+        for j in range(NCHUNK):
+            e, c = divmod(j, 2)
+            w_t = keep.tile([P, 4 * D], BF16, name="w_sb%d" % j)
+            nc.sync.dma_start(
+                out=w_t[:],
+                in_=W_d[e, 512 * c : 512 * c + 512, :].rearrange("(p i) k -> p (i k)", i=4),
+            )
+            w_sb.append(w_t)
+            if c == 0 and e + 1 < E:
+                load_h(e + 1)
 
         low_t = keep.tile([P, 2 * E, P], BF16, name="low_t")
         b_tr = [keep.tile([P, 2, 512], BF16, name="b_tr%d" % e) for e in range(E)]
@@ -75,6 +83,11 @@ def tile_loralinearexpertswrapper_pb_kernel(tc, h, low_d, W_d, B_d, out):
                     nc.tensor.transpose(xl[:, s, :], low_sb[:, e, P * i : P * i + P], ident_bf[:])
                 copy_out(half == 1, low_t[:, 4 * half : 4 * half + 4, :], xl[:])
 
+        def warm_up(n):
+            dummy = accp.tile([P, 512], F32, name="dummy", tag="acc")
+            for d in range(n):
+                nc.tensor.matmul(out=dummy[:], lhsT=zero[:, 0:P], rhs=zero[:], start=True, stop=True)
+
         def b_transposes(e):
             for c in range(2):
                 xb = tp.tile([P, 4, P], BF16, name="xb", tag="tp")
@@ -82,18 +95,18 @@ def tile_loralinearexpertswrapper_pb_kernel(tc, h, low_d, W_d, B_d, out):
                     nc.tensor.transpose(xb[:, i, :], b_sb[e][:, c, P * i : P * i + P], ident_bf[:])
                 copy_out(c == 1, b_tr[e][:, c, :], xb[:].rearrange("p i q -> p (i q)"))
 
-        def lora(e):
-            for c in range(2):
-                for i2 in range(2):
-                    acc = accp.tile([P, 512], F32, name="acc", tag="acc")
-                    nc.tensor.matmul(
-                        out=acc[:], lhsT=low_t[:, 2 * e + i2, :], rhs=b_tr[e][:, c, :], start=True, stop=True
-                    )
-                    copy_out(
-                        i2 == 1,
-                        o_sb[e][:, i2, 512 * c : 512 * c + 512].rearrange("p (q i) -> p q i", i=4),
-                        acc[:].rearrange("p (i q) -> p q i", i=4),
-                    )
+        def lora(j, pool, tag, on_scalar):
+            e, c = divmod(j, 2)
+            for i2 in range(2):
+                acc = pool.tile([P, 512], F32, name="acc", tag=tag)
+                nc.tensor.matmul(
+                    out=acc[:], lhsT=low_t[:, 2 * e + i2, :], rhs=b_tr[e][:, c, :], start=True, stop=True
+                )
+                copy_out(
+                    on_scalar[i2],
+                    o_sb[e][:, i2, 512 * c : 512 * c + 512].rearrange("p (q i) -> p q i", i=4),
+                    acc[:].rearrange("p (i q) -> p q i", i=4),
+                )
 
         def word_transposes(src_f32, tiles_of_bank, g, dst_f32, on_scalar):
             xt = tp.tile([P, 2, 256], F32, name="xt", tag="tp")
@@ -103,13 +116,10 @@ def tile_loralinearexpertswrapper_pb_kernel(tc, h, low_d, W_d, B_d, out):
                     nc.tensor.transpose(xt[:, u, P * s : P * s + P], src_f32[:, col : col + P], ident_f[:])
             copy_out(on_scalar, dst_f32.rearrange("p (n u) -> p n u", u=2), xt[:].rearrange("p u n -> p n u"))
 
-        def h_transposes(e):
-            hg = hgrp_pool.tile([P, 8 * T], BF16, name="hg", align_bytes=64)
-            hgf = hg[:].bitcast(F32)
-            hf = h_sb[e][:].bitcast(F32)
-            for g in range(2):
-                word_transposes(hf, (0, 1), g, hgf[:, 512 * g : 512 * g + 512], True)
-            return hg
+        def h_transposes(e, g, hg, on_scalar):
+            word_transposes(
+                h_sb[e][:].bitcast(F32), (0, 1), g, hg[:].bitcast(F32)[:, 512 * g : 512 * g + 512], on_scalar
+            )
 
         def h_quantise(e, hg):
             nc.vector.quantize_mx(
@@ -118,14 +128,14 @@ def tile_loralinearexpertswrapper_pb_kernel(tc, h, low_d, W_d, B_d, out):
                 in_=hg[:],
             )
 
-        def w_transposes(j):
+        def w_transposes(j, on_scalar):
             grp = grp_pool.tile([P, 4096], BF16, name="grp", align_bytes=64)
             gf = grp[:].bitcast(F32)
             wf = w_sb[j][:].bitcast(F32)
             for g in range(2):
                 for ih in range(2):
                     lo = 1024 * g + 512 * ih
-                    word_transposes(wf, (2 * ih, 2 * ih + 1), g, gf[:, lo : lo + 512], True)
+                    word_transposes(wf, (2 * ih, 2 * ih + 1), g, gf[:, lo : lo + 512], on_scalar[2 * g + ih])
             w_codes = wq_pool.tile([P, 2, 512], U32, name="w_codes", align_bytes=64)
             w_scales = wq_pool.tile([P, 2, 512], U8, name="w_scales", align_bytes=64)
             return grp, w_codes, w_scales
@@ -165,18 +175,24 @@ def tile_loralinearexpertswrapper_pb_kernel(tc, h, low_d, W_d, B_d, out):
         def out_rows(e):
             return out[T * e : T * e + T, :].rearrange("(p i) n -> p i n", i=2)
 
+        warm_up(7)
         low_transposes()
         b_transposes(0)
         b_transposes(1)
-        lora(0)
+        lora(0, accp, "acc", (False, True))
+        lora(1, accp, "acc", (False, True))
         b_transposes(2)
-        lora(1)
+        lora(2, accp, "acc", (False, True))
+        lora(3, accp, "acc", (False, True))
         b_transposes(3)
-        lora(2)
-        hg = h_transposes(0)
-        lora(3)
+        lora(4, accp, "acc", (False, True))
+        lora(5, accp, "acc", (False, True))
+        hg = hgrp_pool.tile([P, 8 * T], BF16, name="hg", align_bytes=64)
+        h_transposes(0, 0, hg, True)
+        h_transposes(0, 1, hg, False)
         h_quantise(0, hg)
-        nxt = w_transposes(0)
+        nxt = w_transposes(0, (True, False, True, False))
+        lora(6, accp, "acc", (True, False))
         w_quantise(nxt, 0)
         w_quantise(nxt, 1)
 
@@ -184,12 +200,16 @@ def tile_loralinearexpertswrapper_pb_kernel(tc, h, low_d, W_d, B_d, out):
             cur = nxt
             e, c = divmod(j, 2)
             if j + 1 < NCHUNK:
-                if c == 1:
-                    hg = h_transposes(e + 1)
-                nxt = w_transposes(j + 1)
-                if c == 1:
+                if e + 1 < E:
+                    if c == 0:
+                        hg = hgrp_pool.tile([P, 8 * T], BF16, name="hg", align_bytes=64)
+                    h_transposes(e + 1, c, hg, True)
+                nxt = w_transposes(j + 1, (True, True, True, True))
+                if e + 1 < E and c == 1:
                     h_quantise(e + 1, hg)
                 w_quantise(nxt, 0)
+            else:
+                lora(7, tp, "tp", (True, True))
             accs = mx_passes(j, cur)
             final_add(j, 0, accs)
             if j + 1 < NCHUNK:

@@ -36,12 +36,19 @@ def tile_loralinearexpertswrapper_pb_kernel(tc, h, low_d, W_d, B_d, out):
         ident_f = keep.tile([P, P], F32, name="ident_f")
         make_identity(nc, ident_f[:])
 
-        low_sb = keep.tile([P, E, 2 * R], BF16, name="low_sb")
-        nc.sync.dma_start(out=low_sb[:], in_=low_d.rearrange("e (p i) r -> p e (i r)", i=2))
+        low_sb = []
         b_sb = []
         for e in range(E):
+            l_t = keep.tile([P, 2 * R], BF16, name="low_sb%d" % e)
+            nc.sync.dma_start(out=l_t[:], in_=low_d[e].rearrange("(p i) r -> p (i r)", i=2))
+            low_sb.append(l_t)
             b_t = keep.tile([P, 2, 4 * R], BF16, name="b_sb%d" % e)
-            nc.sync.dma_start(out=b_t[:], in_=B_d[e].rearrange("(c p i) r -> p c (i r)", c=2, i=4))
+            b_view = B_d[e].rearrange("(c p i) r -> p c (i r)", c=2, i=4)
+            if e == 0:
+                for c in range(2):
+                    nc.sync.dma_start(out=b_t[:, c, :], in_=b_view[:, c, :])
+            else:
+                nc.sync.dma_start(out=b_t[:], in_=b_view)
             b_sb.append(b_t)
         h_sb = []
         w_sb = []
@@ -63,8 +70,7 @@ def tile_loralinearexpertswrapper_pb_kernel(tc, h, low_d, W_d, B_d, out):
             if c == 0 and e + 1 < E:
                 load_h(e + 1)
 
-        low_t = keep.tile([P, 2 * E, P], BF16, name="low_t")
-        b_tr = [keep.tile([P, 2, 512], BF16, name="b_tr%d" % e) for e in range(E)]
+        lora_t = [keep.tile([P, 10, P], BF16, name="lora_t%d" % e) for e in range(E)]
         o_sb = [keep.tile([P, 2, H], F32, name="o_sb%d" % e) for e in range(E)]
         h_codes = [keep.tile([P, 2, T], U32, name="h_codes%d" % e, align_bytes=64) for e in range(E)]
         h_scales = [keep.tile([P, 2, T], U8, name="h_scales%d" % e, align_bytes=64) for e in range(E)]
@@ -75,32 +81,33 @@ def tile_loralinearexpertswrapper_pb_kernel(tc, h, low_d, W_d, B_d, out):
             else:
                 nc.vector.tensor_copy(out=dst, in_=src)
 
-        def low_transposes():
-            for half in range(2):
-                xl = tp.tile([P, 4, P], BF16, name="xl", tag="tp")
-                for s in range(4):
-                    e, i = divmod(4 * half + s, 2)
-                    nc.tensor.transpose(xl[:, s, :], low_sb[:, e, P * i : P * i + P], ident_bf[:])
-                copy_out(half == 1, low_t[:, 4 * half : 4 * half + 4, :], xl[:])
-
         def warm_up(n):
             dummy = accp.tile([P, 512], F32, name="dummy", tag="acc")
             for d in range(n):
                 nc.tensor.matmul(out=dummy[:], lhsT=zero[:, 0:P], rhs=zero[:], start=True, stop=True)
 
         def b_transposes(e):
-            for c in range(2):
-                xb = tp.tile([P, 4, P], BF16, name="xb", tag="tp")
-                for i in range(4):
-                    nc.tensor.transpose(xb[:, i, :], b_sb[e][:, c, P * i : P * i + P], ident_bf[:])
-                copy_out(c == 1, b_tr[e][:, c, :], xb[:].rearrange("p i q -> p (i q)"))
+            xa = tp.tile([P, 6, P], BF16, name="xa", tag="tp")
+            for i in range(2):
+                nc.tensor.transpose(xa[:, i, :], low_sb[e][:, P * i : P * i + P], ident_bf[:])
+            for i in range(4):
+                nc.tensor.transpose(xa[:, 2 + i, :], b_sb[e][:, 0, P * i : P * i + P], ident_bf[:])
+            copy_out(False, lora_t[e][:, 0:6, :], xa[:])
+            xb = tp.tile([P, 4, P], BF16, name="xb", tag="tp")
+            for i in range(4):
+                nc.tensor.transpose(xb[:, i, :], b_sb[e][:, 1, P * i : P * i + P], ident_bf[:])
+            copy_out(True, lora_t[e][:, 6:10, :], xb[:])
 
         def lora(j, pool, tag, on_scalar):
             e, c = divmod(j, 2)
             for i2 in range(2):
                 acc = pool.tile([P, 512], F32, name="acc", tag=tag)
                 nc.tensor.matmul(
-                    out=acc[:], lhsT=low_t[:, 2 * e + i2, :], rhs=b_tr[e][:, c, :], start=True, stop=True
+                    out=acc[:],
+                    lhsT=lora_t[e][:, i2, :],
+                    rhs=lora_t[e][:, 2 + 4 * c : 6 + 4 * c, :].rearrange("p i q -> p (i q)"),
+                    start=True,
+                    stop=True,
                 )
                 copy_out(
                     on_scalar[i2],
@@ -175,8 +182,7 @@ def tile_loralinearexpertswrapper_pb_kernel(tc, h, low_d, W_d, B_d, out):
         def out_rows(e):
             return out[T * e : T * e + T, :].rearrange("(p i) n -> p i n", i=2)
 
-        warm_up(7)
-        low_transposes()
+        warm_up(6)
         b_transposes(0)
         b_transposes(1)
         lora(0, accp, "acc", (False, True))

@@ -27,7 +27,6 @@ def tile_loralinearexpertswrapper_pb_kernel(tc, h, low_d, W_d, B_d, out):
         wq_pool = ctx.enter_context(tc.tile_pool(name="wq", bufs=3))
         tp = ctx.enter_context(tc.psum_pool(name="tp", bufs=4))
         accp = ctx.enter_context(tc.psum_pool(name="accp", bufs=4))
-        ctx.enter_context(tc.manual_schedule())
 
         zero = keep.tile([P, 512], BF16, name="zero")
         nc.vector.memset(zero[:], 0.0)

@@ -27,6 +27,7 @@ def tile_loralinearexpertswrapper_pb_kernel(tc, h, low_d, W_d, B_d, out):
         wq_pool = ctx.enter_context(tc.tile_pool(name="wq", bufs=3))
         tp = ctx.enter_context(tc.psum_pool(name="tp", bufs=4))
         accp = ctx.enter_context(tc.psum_pool(name="accp", bufs=4))
+        ctx.enter_context(tc.manual_schedule())
 
         zero = keep.tile([P, 512], BF16, name="zero")
         nc.vector.memset(zero[:], 0.0)
@@ -194,10 +195,10 @@ def tile_loralinearexpertswrapper_pb_kernel(tc, h, low_d, W_d, B_d, out):
         lora(5, accp, "acc", (False, True))
         hg = hgrp_pool.tile([P, 8 * T], BF16, name="hg", align_bytes=64)
         h_transposes(0, 0, hg, True)
-        h_transposes(0, 1, hg, False)
+        h_transposes(0, 1, hg, True)
         h_quantise(0, hg)
         nxt = w_transposes(0, (True, False, True, False))
-        lora(6, accp, "acc", (True, False))
+        lora(6, accp, "acc", (True, True))
         w_quantise(nxt, 0)
         w_quantise(nxt, 1)
 

@@ -16,6 +16,8 @@ E, T, H, D, R = 4, 256, 1024, 1024, 128
 SCALE = 2.0
 FLOPS = 2 * E * T * H * (D + R)
 NCHUNK = 2 * E
+HEAD_T, MAIN_T, N_HEAD_T = (0, 1, 2, 3), (4, 2, 3, 0, 1), 14
+HEAD_P, MAIN_P, N_HEAD_P = (4, 5, 6, 7), (7, 5, 6), 15
 
 
 def tile_loralinearexpertswrapper_pb_kernel(tc, h, low_d, W_d, B_d, out):
@@ -25,8 +27,7 @@ def tile_loralinearexpertswrapper_pb_kernel(tc, h, low_d, W_d, B_d, out):
         grp_pool = ctx.enter_context(tc.tile_pool(name="grp", bufs=3))
         hgrp_pool = ctx.enter_context(tc.tile_pool(name="hgrp", bufs=2))
         wq_pool = ctx.enter_context(tc.tile_pool(name="wq", bufs=3))
-        tp = ctx.enter_context(tc.psum_pool(name="tp", bufs=4))
-        accp = ctx.enter_context(tc.psum_pool(name="accp", bufs=4))
+        psum = ctx.enter_context(tc.psum_pool(name="psum", bufs=1))
         ctx.enter_context(tc.manual_schedule())
 
         zero = keep.tile([P, 512], BF16, name="zero")
@@ -75,6 +76,20 @@ def tile_loralinearexpertswrapper_pb_kernel(tc, h, low_d, W_d, B_d, out):
         h_codes = [keep.tile([P, 2, T], U32, name="h_codes%d" % e, align_bytes=64) for e in range(E)]
         h_scales = [keep.tile([P, 2, T], U8, name="h_scales%d" % e, align_bytes=64) for e in range(E)]
 
+        taken = [0, 0]
+
+        def transpose_tile(shape, dtype, name):
+            n = taken[0]
+            taken[0] = n + 1
+            bank = HEAD_T[n % 4] if n < N_HEAD_T else MAIN_T[(n - N_HEAD_T) % 5]
+            return psum.tile(shape, dtype, name=name, tag="bank%d" % bank)
+
+        def product_tile(name):
+            n = taken[1]
+            taken[1] = n + 1
+            bank = HEAD_P[n % 4] if n < N_HEAD_P else MAIN_P[(n - N_HEAD_P) % 3]
+            return psum.tile([P, 512], F32, name=name, tag="bank%d" % bank)
+
         def copy_out(on_scalar, dst, src):
             if on_scalar:
                 nc.scalar.copy(out=dst, in_=src)
@@ -82,26 +97,26 @@ def tile_loralinearexpertswrapper_pb_kernel(tc, h, low_d, W_d, B_d, out):
                 nc.vector.tensor_copy(out=dst, in_=src)
 
         def warm_up(n):
-            dummy = accp.tile([P, 512], F32, name="dummy", tag="acc")
+            dummy = product_tile("dummy")
             for d in range(n):
                 nc.tensor.matmul(out=dummy[:], lhsT=zero[:, 0:P], rhs=zero[:], start=True, stop=True)
 
         def b_transposes(e):
-            xa = tp.tile([P, 6, P], BF16, name="xa", tag="tp")
+            xa = transpose_tile([P, 6, P], BF16, "xa")
             for i in range(2):
                 nc.tensor.transpose(xa[:, i, :], low_sb[e][:, P * i : P * i + P], ident_bf[:])
             for i in range(4):
                 nc.tensor.transpose(xa[:, 2 + i, :], b_sb[e][:, 0, P * i : P * i + P], ident_bf[:])
             copy_out(False, lora_t[e][:, 0:6, :], xa[:])
-            xb = tp.tile([P, 4, P], BF16, name="xb", tag="tp")
+            xb = transpose_tile([P, 4, P], BF16, "xb")
             for i in range(4):
                 nc.tensor.transpose(xb[:, i, :], b_sb[e][:, 1, P * i : P * i + P], ident_bf[:])
             copy_out(True, lora_t[e][:, 6:10, :], xb[:])
 
-        def lora(j, pool, tag, on_scalar):
+        def lora(j, among_transposes, on_scalar):
             e, c = divmod(j, 2)
             for i2 in range(2):
-                acc = pool.tile([P, 512], F32, name="acc", tag=tag)
+                acc = transpose_tile([P, 512], F32, "acc") if among_transposes else product_tile("acc")
                 nc.tensor.matmul(
                     out=acc[:],
                     lhsT=lora_t[e][:, i2, :],
@@ -116,7 +131,7 @@ def tile_loralinearexpertswrapper_pb_kernel(tc, h, low_d, W_d, B_d, out):
                 )
 
         def word_transposes(src_f32, tiles_of_bank, g, dst_f32, on_scalar):
-            xt = tp.tile([P, 2, 256], F32, name="xt", tag="tp")
+            xt = transpose_tile([P, 2, 256], F32, "xt")
             for u in range(2):
                 for s in range(2):
                     col = 512 * tiles_of_bank[s] + 256 * g + P * u
@@ -158,7 +173,7 @@ def tile_loralinearexpertswrapper_pb_kernel(tc, h, low_d, W_d, B_d, out):
         def mx_passes(j, st):
             e = j // 2
             w_codes, w_scales = st[1], st[2]
-            accs = [accp.tile([P, 512], F32, name="macc%d" % i2, tag="acc") for i2 in range(2)]
+            accs = [product_tile("macc%d" % i2) for i2 in range(2)]
             for g in range(2):
                 for i2 in range(2):
                     nc.tensor.matmul_mx(
@@ -185,20 +200,20 @@ def tile_loralinearexpertswrapper_pb_kernel(tc, h, low_d, W_d, B_d, out):
         warm_up(6)
         b_transposes(0)
         b_transposes(1)
-        lora(0, accp, "acc", (False, True))
-        lora(1, accp, "acc", (False, True))
+        lora(0, False, (False, True))
+        lora(1, False, (False, True))
         b_transposes(2)
-        lora(2, accp, "acc", (False, True))
-        lora(3, accp, "acc", (False, True))
+        lora(2, False, (False, True))
+        lora(3, False, (False, True))
         b_transposes(3)
-        lora(4, accp, "acc", (False, True))
-        lora(5, accp, "acc", (False, True))
+        lora(4, False, (False, True))
+        lora(5, False, (False, True))
         hg = hgrp_pool.tile([P, 8 * T], BF16, name="hg", align_bytes=64)
         h_transposes(0, 0, hg, True)
-        h_transposes(0, 1, hg, True)
+        h_transposes(0, 1, hg, False)
         h_quantise(0, hg)
         nxt = w_transposes(0, (True, False, True, False))
-        lora(6, accp, "acc", (True, True))
+        lora(6, False, (True, False))
         w_quantise(nxt, 0)
         w_quantise(nxt, 1)
 
@@ -215,7 +230,7 @@ def tile_loralinearexpertswrapper_pb_kernel(tc, h, low_d, W_d, B_d, out):
                     h_quantise(e + 1, hg)
                 w_quantise(nxt, 0)
             else:
-                lora(7, tp, "tp", (True, True))
+                lora(7, True, (True, True))
             accs = mx_passes(j, cur)
             final_add(j, 0, accs)
             if j + 1 < NCHUNK:

@@ -72,7 +72,7 @@ def tile_loralinearexpertswrapper_pb_kernel(tc, h, low_d, W_d, B_d, out):
                 load_h(e + 1)
 
         lora_t = [keep.tile([P, 10, P], BF16, name="lora_t%d" % e) for e in range(E)]
-        o_sb = [keep.tile([P, 2, H], F32, name="o_sb%d" % e) for e in range(E)]
+        o_sb = [keep.tile([P, 2, 512], F32, name="o_sb%d" % j) for j in range(NCHUNK)]
         h_codes = [keep.tile([P, 2, T], U32, name="h_codes%d" % e, align_bytes=64) for e in range(E)]
         h_scales = [keep.tile([P, 2, T], U8, name="h_scales%d" % e, align_bytes=64) for e in range(E)]
 
@@ -126,7 +126,7 @@ def tile_loralinearexpertswrapper_pb_kernel(tc, h, low_d, W_d, B_d, out):
                 )
                 copy_out(
                     on_scalar[i2],
-                    o_sb[e][:, i2, 512 * c : 512 * c + 512].rearrange("p (q i) -> p q i", i=4),
+                    o_sb[j][:, i2, :].rearrange("p (q i) -> p q i", i=4),
                     acc[:].rearrange("p (i q) -> p q i", i=4),
                 )
 
@@ -188,14 +188,14 @@ def tile_loralinearexpertswrapper_pb_kernel(tc, h, low_d, W_d, B_d, out):
             return accs
 
         def final_add(j, i2, accs):
-            e, c = divmod(j, 2)
-            dst = o_sb[e][:, i2, 512 * c : 512 * c + 512].rearrange("p (q i) -> p q i", i=4)
+            dst = o_sb[j][:, i2, :].rearrange("p (q i) -> p q i", i=4)
             nc.vector.scalar_tensor_tensor(
                 out=dst, in0=dst, scalar=SCALE, in1=accs[i2][:].rearrange("p (i q) -> p q i", i=4), op0=MULT, op1=ADD
             )
 
-        def out_rows(e):
-            return out[T * e : T * e + T, :].rearrange("(p i) n -> p i n", i=2)
+        def out_part(j):
+            e, c = divmod(j, 2)
+            return out[T * e : T * e + T, 512 * c : 512 * c + 512].rearrange("(p i) n -> p i n", i=2)
 
         warm_up(6)
         b_transposes(0)
@@ -236,11 +236,9 @@ def tile_loralinearexpertswrapper_pb_kernel(tc, h, low_d, W_d, B_d, out):
             if j + 1 < NCHUNK:
                 w_quantise(nxt, 1)
             if j == NCHUNK - 1:
-                nc.sync.dma_start(out=out_rows(e)[:, 0, 512:1024], in_=o_sb[e][:, 0, 512:1024])
+                nc.sync.dma_start(out=out_part(j)[:, 0, :], in_=o_sb[j][:, 0, :])
             final_add(j, 1, accs)
             if j == NCHUNK - 1:
-                nc.sync.dma_start(out=out_rows(e)[:, 1, 512:1024], in_=o_sb[e][:, 1, 512:1024])
-            elif j == NCHUNK - 2:
-                nc.sync.dma_start(out=out_rows(e)[:, :, 0:512], in_=o_sb[e][:, :, 0:512])
-            elif c == 1:
-                nc.sync.dma_start(out=out_rows(e), in_=o_sb[e][:])
+                nc.sync.dma_start(out=out_part(j)[:, 1, :], in_=o_sb[j][:, 1, :])
+            else:
+                nc.sync.dma_start(out=out_part(j), in_=o_sb[j][:])

@@ -16,8 +16,7 @@ E, T, H, D, R = 4, 256, 1024, 1024, 128
 SCALE = 2.0
 FLOPS = 2 * E * T * H * (D + R)
 NCHUNK = 2 * E
-HEAD_T, MAIN_T, N_HEAD_T = (0, 1, 2, 3), (4, 2, 3, 0, 1), 14
-HEAD_P, MAIN_P, N_HEAD_P = (4, 5, 6, 7), (7, 5, 6), 15
+T_BANKS = 4
 
 
 def tile_loralinearexpertswrapper_pb_kernel(tc, h, low_d, W_d, B_d, out):
@@ -81,14 +80,12 @@ def tile_loralinearexpertswrapper_pb_kernel(tc, h, low_d, W_d, B_d, out):
         def transpose_tile(shape, dtype, name):
             n = taken[0]
             taken[0] = n + 1
-            bank = HEAD_T[n % 4] if n < N_HEAD_T else MAIN_T[(n - N_HEAD_T) % 5]
-            return psum.tile(shape, dtype, name=name, tag="bank%d" % bank)
+            return psum.tile(shape, dtype, name=name, tag="bank%d" % (n % T_BANKS))
 
         def product_tile(name):
             n = taken[1]
             taken[1] = n + 1
-            bank = HEAD_P[n % 4] if n < N_HEAD_P else MAIN_P[(n - N_HEAD_P) % 3]
-            return psum.tile([P, 512], F32, name=name, tag="bank%d" % bank)
+            return psum.tile([P, 512], F32, name=name, tag="bank%d" % (T_BANKS + n % (8 - T_BANKS)))
 
         def copy_out(on_scalar, dst, src):
             if on_scalar:
@@ -143,24 +140,25 @@ def tile_loralinearexpertswrapper_pb_kernel(tc, h, low_d, W_d, B_d, out):
                 h_sb[e][:].bitcast(F32), (0, 1), g, hg[:].bitcast(F32)[:, 512 * g : 512 * g + 512], on_scalar
             )
 
-        def h_quantise(e, hg):
+        def h_quantise(e, g, hg):
             nc.vector.quantize_mx(
-                out=h_codes[e][:].rearrange("p g n -> p (g n)").bitcast(FP8X4),
-                scales=h_scales[e][:].rearrange("p g n -> p (g n)"),
-                in_=hg[:],
+                out=h_codes[e][:, g, :].bitcast(FP8X4),
+                scales=h_scales[e][:, g, :],
+                in_=hg[:, 4 * T * g : 4 * T * g + 4 * T],
             )
 
-        def w_transposes(j, on_scalar):
+        def w_tiles():
             grp = grp_pool.tile([P, 4096], BF16, name="grp", align_bytes=64)
-            gf = grp[:].bitcast(F32)
-            wf = w_sb[j][:].bitcast(F32)
-            for g in range(2):
-                for ih in range(2):
-                    lo = 1024 * g + 512 * ih
-                    word_transposes(wf, (2 * ih, 2 * ih + 1), g, gf[:, lo : lo + 512], on_scalar[2 * g + ih])
             w_codes = wq_pool.tile([P, 2, 512], U32, name="w_codes", align_bytes=64)
             w_scales = wq_pool.tile([P, 2, 512], U8, name="w_scales", align_bytes=64)
             return grp, w_codes, w_scales
+
+        def w_transposes(j, g, st, on_scalar):
+            gf = st[0][:].bitcast(F32)
+            wf = w_sb[j][:].bitcast(F32)
+            for ih in range(2):
+                lo = 1024 * g + 512 * ih
+                word_transposes(wf, (2 * ih, 2 * ih + 1), g, gf[:, lo : lo + 512], on_scalar[ih])
 
         def w_quantise(st, g):
             grp, w_codes, w_scales = st
@@ -170,22 +168,19 @@ def tile_loralinearexpertswrapper_pb_kernel(tc, h, low_d, W_d, B_d, out):
                 in_=grp[:, 2048 * g : 2048 * g + 2048],
             )
 
-        def mx_passes(j, st):
+        def mx_passes(j, g, st, accs):
             e = j // 2
             w_codes, w_scales = st[1], st[2]
-            accs = [product_tile("macc%d" % i2) for i2 in range(2)]
-            for g in range(2):
-                for i2 in range(2):
-                    nc.tensor.matmul_mx(
-                        out=accs[i2][:],
-                        lhsT=h_codes[e][:, g, P * i2 : P * i2 + P].bitcast(FP8X4),
-                        lhsT_scale=h_scales[e][:, g, P * i2 : P * i2 + P],
-                        rhs=w_codes[:, g, :].bitcast(FP8X4),
-                        rhs_scale=w_scales[:, g, :],
-                        start=(g == 0),
-                        stop=(g == 1),
-                    )
-            return accs
+            for i2 in range(2):
+                nc.tensor.matmul_mx(
+                    out=accs[i2][:],
+                    lhsT=h_codes[e][:, g, P * i2 : P * i2 + P].bitcast(FP8X4),
+                    lhsT_scale=h_scales[e][:, g, P * i2 : P * i2 + P],
+                    rhs=w_codes[:, g, :].bitcast(FP8X4),
+                    rhs_scale=w_scales[:, g, :],
+                    start=(g == 0),
+                    stop=(g == 1),
+                )
 
         def final_add(j, i2, accs):
             dst = o_sb[j][:, i2, :].rearrange("p (q i) -> p q i", i=4)
@@ -211,34 +206,42 @@ def tile_loralinearexpertswrapper_pb_kernel(tc, h, low_d, W_d, B_d, out):
         hg = hgrp_pool.tile([P, 8 * T], BF16, name="hg", align_bytes=64)
         h_transposes(0, 0, hg, True)
         h_transposes(0, 1, hg, False)
-        h_quantise(0, hg)
-        nxt = w_transposes(0, (True, False, True, False))
+        h_quantise(0, 0, hg)
+        h_quantise(0, 1, hg)
+        nxt = w_tiles()
+        w_transposes(0, 0, nxt, (True, False))
+        w_transposes(0, 1, nxt, (True, False))
         lora(6, False, (True, False))
         w_quantise(nxt, 0)
-        w_quantise(nxt, 1)
 
+        last = None
         for j in range(NCHUNK):
             cur = nxt
             e, c = divmod(j, 2)
+            if j > 0:
+                final_add(j - 1, 0, last)
+            w_quantise(cur, 1)
+            if j > 0:
+                final_add(j - 1, 1, last)
+                nc.sync.dma_start(out=out_part(j - 1), in_=o_sb[j - 1][:])
+            accs = [product_tile("macc%d" % i2) for i2 in range(2)]
             if j + 1 < NCHUNK:
+                nxt = w_tiles()
                 if e + 1 < E:
                     if c == 0:
                         hg = hgrp_pool.tile([P, 8 * T], BF16, name="hg", align_bytes=64)
                     h_transposes(e + 1, c, hg, True)
-                nxt = w_transposes(j + 1, (True, True, True, True))
-                if e + 1 < E and c == 1:
-                    h_quantise(e + 1, hg)
-                w_quantise(nxt, 0)
+                w_transposes(j + 1, 0, nxt, (True, True))
             else:
                 lora(7, True, (True, True))
-            accs = mx_passes(j, cur)
-            final_add(j, 0, accs)
+            mx_passes(j, 0, cur, accs)
             if j + 1 < NCHUNK:
-                w_quantise(nxt, 1)
-            if j == NCHUNK - 1:
-                nc.sync.dma_start(out=out_part(j)[:, 0, :], in_=o_sb[j][:, 0, :])
-            final_add(j, 1, accs)
-            if j == NCHUNK - 1:
-                nc.sync.dma_start(out=out_part(j)[:, 1, :], in_=o_sb[j][:, 1, :])
-            else:
-                nc.sync.dma_start(out=out_part(j), in_=o_sb[j][:])
+                if e + 1 < E:
+                    h_quantise(e + 1, c, hg)
+                w_quantise(nxt, 0)
+                w_transposes(j + 1, 1, nxt, (True, True))
+            mx_passes(j, 1, cur, accs)
+            last = accs
+        for i2 in range(2):
+            final_add(NCHUNK - 1, i2, last)
+            nc.sync.dma_start(out=out_part(NCHUNK - 1)[:, i2, :], in_=o_sb[NCHUNK - 1][:, i2, :])

@@ -8,14 +8,14 @@ BF16 = mybir.dt.bfloat16
 U32 = mybir.dt.uint32
 U8 = mybir.dt.uint8
 FP8X4 = mybir.dt.float8_e4m3fn_x4
-MULT = mybir.AluOpType.mult
-ADD = mybir.AluOpType.add
 
 P = 128
 E, T, H, D, R = 4, 256, 1024, 1024, 128
 SCALE = 2.0
 FLOPS = 2 * E * T * H * (D + R)
-NCHUNK = 2 * E
+UN = 256
+UPE = H // UN
+NU = E * UPE
 T_BANKS = 4
 
 
@@ -23,9 +23,9 @@ def tile_loralinearexpertswrapper_pb_kernel(tc, h, low_d, W_d, B_d, out):
     nc = tc.nc
     with ExitStack() as ctx:
         keep = ctx.enter_context(tc.tile_pool(name="keep", bufs=1))
-        grp_pool = ctx.enter_context(tc.tile_pool(name="grp", bufs=3))
+        grp_pool = ctx.enter_context(tc.tile_pool(name="grp", bufs=4))
         hgrp_pool = ctx.enter_context(tc.tile_pool(name="hgrp", bufs=2))
-        wq_pool = ctx.enter_context(tc.tile_pool(name="wq", bufs=3))
+        wq_pool = ctx.enter_context(tc.tile_pool(name="wq", bufs=4))
         psum = ctx.enter_context(tc.psum_pool(name="psum", bufs=1))
         ctx.enter_context(tc.manual_schedule())
 
@@ -42,13 +42,8 @@ def tile_loralinearexpertswrapper_pb_kernel(tc, h, low_d, W_d, B_d, out):
             l_t = keep.tile([P, 2 * R], BF16, name="low_sb%d" % e)
             nc.sync.dma_start(out=l_t[:], in_=low_d[e].rearrange("(p i) r -> p (i r)", i=2))
             low_sb.append(l_t)
-            b_t = keep.tile([P, 2, 4 * R], BF16, name="b_sb%d" % e)
-            b_view = B_d[e].rearrange("(c p i) r -> p c (i r)", c=2, i=4)
-            if e == 0:
-                for c in range(2):
-                    nc.sync.dma_start(out=b_t[:, c, :], in_=b_view[:, c, :])
-            else:
-                nc.sync.dma_start(out=b_t[:], in_=b_view)
+            b_t = keep.tile([P, 8 * R], BF16, name="b_sb%d" % e)
+            nc.sync.dma_start(out=b_t[:], in_=B_d[e].rearrange("(p i) r -> p (i r)", i=8))
             b_sb.append(b_t)
         h_sb = []
         w_sb = []
@@ -59,19 +54,19 @@ def tile_loralinearexpertswrapper_pb_kernel(tc, h, low_d, W_d, B_d, out):
             h_sb.append(h_t)
 
         load_h(0)
-        for j in range(NCHUNK):
-            e, c = divmod(j, 2)
-            w_t = keep.tile([P, 4 * D], BF16, name="w_sb%d" % j)
+        for u in range(NU):
+            e, s = divmod(u, UPE)
+            w_t = keep.tile([P, 2 * D], BF16, name="w_sb%d" % u)
             nc.sync.dma_start(
-                out=w_t[:],
-                in_=W_d[e, 512 * c : 512 * c + 512, :].rearrange("(p i) k -> p (i k)", i=4),
+                out=w_t[:], in_=W_d[e, UN * s : UN * s + UN, :].rearrange("(p i) k -> p (i k)", i=2)
             )
             w_sb.append(w_t)
-            if c == 0 and e + 1 < E:
+            if s == 1 and e + 1 < E:
                 load_h(e + 1)
 
         lora_t = [keep.tile([P, 10, P], BF16, name="lora_t%d" % e) for e in range(E)]
-        o_sb = [keep.tile([P, 2, 512], F32, name="o_sb%d" % j) for j in range(NCHUNK)]
+        o_sb = [keep.tile([P, 2, H], F32, name="o_sb%d" % e) for e in range(E - 1)]
+        o_last = keep.tile([P, UPE, 2, UN], F32, name="o_last")
         h_codes = [keep.tile([P, 2, T], U32, name="h_codes%d" % e, align_bytes=64) for e in range(E)]
         h_scales = [keep.tile([P, 2, T], U8, name="h_scales%d" % e, align_bytes=64) for e in range(E)]
 
@@ -103,145 +98,147 @@ def tile_loralinearexpertswrapper_pb_kernel(tc, h, low_d, W_d, B_d, out):
             for i in range(2):
                 nc.tensor.transpose(xa[:, i, :], low_sb[e][:, P * i : P * i + P], ident_bf[:])
             for i in range(4):
-                nc.tensor.transpose(xa[:, 2 + i, :], b_sb[e][:, 0, P * i : P * i + P], ident_bf[:])
+                nc.tensor.transpose(xa[:, 2 + i, :], b_sb[e][:, P * i : P * i + P], ident_bf[:])
             copy_out(False, lora_t[e][:, 0:6, :], xa[:])
             xb = transpose_tile([P, 4, P], BF16, "xb")
             for i in range(4):
-                nc.tensor.transpose(xb[:, i, :], b_sb[e][:, 1, P * i : P * i + P], ident_bf[:])
+                nc.tensor.transpose(xb[:, i, :], b_sb[e][:, P * (4 + i) : P * (4 + i) + P], ident_bf[:])
             copy_out(True, lora_t[e][:, 6:10, :], xb[:])
 
-        def lora(j, among_transposes, on_scalar):
-            e, c = divmod(j, 2)
-            for i2 in range(2):
-                acc = transpose_tile([P, 512], F32, "acc") if among_transposes else product_tile("acc")
-                nc.tensor.matmul(
-                    out=acc[:],
-                    lhsT=lora_t[e][:, i2, :],
-                    rhs=lora_t[e][:, 2 + 4 * c : 6 + 4 * c, :].rearrange("p i q -> p (i q)"),
-                    start=True,
-                    stop=True,
-                )
-                copy_out(
-                    on_scalar[i2],
-                    o_sb[j][:, i2, :].rearrange("p (q i) -> p q i", i=4),
-                    acc[:].rearrange("p (i q) -> p q i", i=4),
-                )
+        def lora(e, c, i2, on_scalar):
+            acc = product_tile("acc")
+            nc.tensor.matmul(
+                out=acc[:],
+                lhsT=lora_t[e][:, i2, :],
+                rhs=lora_t[e][:, 2 + 4 * c : 6 + 4 * c, :].rearrange("p i q -> p (i q)"),
+                start=True,
+                stop=True,
+            )
+            if e < E - 1:
+                dst = o_sb[e][:, i2, :].rearrange("p (q i) -> p q i", i=8)[:, :, 4 * c : 4 * c + 4]
+                src = acc[:].rearrange("p (i q) -> p q i", i=4)
+            else:
+                dst = o_last[:, :, i2, :].rearrange("p s (q i) -> p s q i", i=8)[:, :, :, 4 * c : 4 * c + 4]
+                src = acc[:].rearrange("p (i s q) -> p s q i", i=4, s=UPE)
+            if on_scalar:
+                nc.scalar.mul(out=dst, in_=src, mul=SCALE)
+            else:
+                nc.vector.tensor_scalar_mul(out=dst, in0=src, scalar1=SCALE)
 
-        def word_transposes(src_f32, tiles_of_bank, g, dst_f32, on_scalar):
+        def word_transposes(src_f32, g, dst_f32, on_scalar):
             xt = transpose_tile([P, 2, 256], F32, "xt")
             for u in range(2):
-                for s in range(2):
-                    col = 512 * tiles_of_bank[s] + 256 * g + P * u
-                    nc.tensor.transpose(xt[:, u, P * s : P * s + P], src_f32[:, col : col + P], ident_f[:])
+                for i in range(2):
+                    col = 512 * i + 256 * g + P * u
+                    nc.tensor.transpose(xt[:, u, P * i : P * i + P], src_f32[:, col : col + P], ident_f[:])
             copy_out(on_scalar, dst_f32.rearrange("p (n u) -> p n u", u=2), xt[:].rearrange("p u n -> p n u"))
 
-        def h_transposes(e, g, hg, on_scalar):
+        h_grp = {}
+
+        def h_transposes(e, g, on_scalar):
+            if g == 0:
+                h_grp[e] = hgrp_pool.tile([P, 8 * T], BF16, name="hg", align_bytes=64)
             word_transposes(
-                h_sb[e][:].bitcast(F32), (0, 1), g, hg[:].bitcast(F32)[:, 512 * g : 512 * g + 512], on_scalar
+                h_sb[e][:].bitcast(F32), g, h_grp[e][:].bitcast(F32)[:, 512 * g : 512 * g + 512], on_scalar
             )
 
-        def h_quantise(e, g, hg):
+        def h_quantise(e):
             nc.vector.quantize_mx(
-                out=h_codes[e][:, g, :].bitcast(FP8X4),
-                scales=h_scales[e][:, g, :],
-                in_=hg[:, 4 * T * g : 4 * T * g + 4 * T],
+                out=h_codes[e][:].rearrange("p g n -> p (g n)").bitcast(FP8X4),
+                scales=h_scales[e][:].rearrange("p g n -> p (g n)"),
+                in_=h_grp[e][:],
             )
 
-        def w_tiles():
-            grp = grp_pool.tile([P, 4096], BF16, name="grp", align_bytes=64)
-            w_codes = wq_pool.tile([P, 2, 512], U32, name="w_codes", align_bytes=64)
-            w_scales = wq_pool.tile([P, 2, 512], U8, name="w_scales", align_bytes=64)
-            return grp, w_codes, w_scales
+        w_st = {}
 
-        def w_transposes(j, g, st, on_scalar):
-            gf = st[0][:].bitcast(F32)
-            wf = w_sb[j][:].bitcast(F32)
-            for ih in range(2):
-                lo = 1024 * g + 512 * ih
-                word_transposes(wf, (2 * ih, 2 * ih + 1), g, gf[:, lo : lo + 512], on_scalar[ih])
+        def w_transposes(u, g, on_scalar):
+            if g == 0:
+                grp = grp_pool.tile([P, 2048], BF16, name="grp", align_bytes=64)
+                w_codes = wq_pool.tile([P, 2, UN], U32, name="w_codes", align_bytes=64)
+                w_scales = wq_pool.tile([P, 2, UN], U8, name="w_scales", align_bytes=64)
+                w_st[u] = (grp, w_codes, w_scales)
+            word_transposes(
+                w_sb[u][:].bitcast(F32), g, w_st[u][0][:].bitcast(F32)[:, 512 * g : 512 * g + 512], on_scalar
+            )
 
-        def w_quantise(st, g):
-            grp, w_codes, w_scales = st
+        def w_quantise(u):
+            grp, w_codes, w_scales = w_st[u]
             nc.vector.quantize_mx(
-                out=w_codes[:, g, :].bitcast(FP8X4),
-                scales=w_scales[:, g, :],
-                in_=grp[:, 2048 * g : 2048 * g + 2048],
+                out=w_codes[:].rearrange("p g n -> p (g n)").bitcast(FP8X4),
+                scales=w_scales[:].rearrange("p g n -> p (g n)"),
+                in_=grp[:],
             )
 
-        def mx_passes(j, g, st, accs):
-            e = j // 2
-            w_codes, w_scales = st[1], st[2]
+        accs = {}
+
+        def mx_passes(u):
+            e = u // UPE
+            grp, w_codes, w_scales = w_st[u]
+            accs[u] = product_tile("macc")
             for i2 in range(2):
-                nc.tensor.matmul_mx(
-                    out=accs[i2][:],
-                    lhsT=h_codes[e][:, g, P * i2 : P * i2 + P].bitcast(FP8X4),
-                    lhsT_scale=h_scales[e][:, g, P * i2 : P * i2 + P],
-                    rhs=w_codes[:, g, :].bitcast(FP8X4),
-                    rhs_scale=w_scales[:, g, :],
-                    start=(g == 0),
-                    stop=(g == 1),
-                )
+                for g in range(2):
+                    nc.tensor.matmul_mx(
+                        out=accs[u][:, UN * i2 : UN * i2 + UN],
+                        lhsT=h_codes[e][:, g, P * i2 : P * i2 + P].bitcast(FP8X4),
+                        lhsT_scale=h_scales[e][:, g, P * i2 : P * i2 + P],
+                        rhs=w_codes[:, g, :].bitcast(FP8X4),
+                        rhs_scale=w_scales[:, g, :],
+                        start=(g == 0),
+                        stop=(g == 1),
+                    )
 
-        def final_add(j, i2, accs):
-            dst = o_sb[j][:, i2, :].rearrange("p (q i) -> p q i", i=4)
-            nc.vector.scalar_tensor_tensor(
-                out=dst, in0=dst, scalar=SCALE, in1=accs[i2][:].rearrange("p (i q) -> p q i", i=4), op0=MULT, op1=ADD
-            )
+        def final_add(u):
+            e, s = divmod(u, UPE)
+            part = o_sb[e][:, :, UN * s : UN * s + UN] if e < E - 1 else o_last[:, s, :, :]
+            dst = part.rearrange("p t (q i) -> p t q i", i=2)
+            nc.vector.tensor_add(out=dst, in0=dst, in1=accs[u][:].rearrange("p (t i q) -> p t q i", t=2, i=2))
 
-        def out_part(j):
-            e, c = divmod(j, 2)
-            return out[T * e : T * e + T, 512 * c : 512 * c + 512].rearrange("(p i) n -> p i n", i=2)
+        def store(u):
+            e, s = divmod(u, UPE)
+            rows = out[T * e : T * e + T, :].rearrange("(p i) n -> p i n", i=2)
+            if e == E - 1:
+                nc.sync.dma_start(out=rows[:, :, UN * s : UN * s + UN], in_=o_last[:, s, :, :])
+            elif s == UPE - 1:
+                nc.sync.dma_start(out=rows, in_=o_sb[e][:])
 
         warm_up(6)
         b_transposes(0)
         b_transposes(1)
-        lora(0, False, (False, True))
-        lora(1, False, (False, True))
+        for i in range(4):
+            lora(0, i // 2, i % 2, i % 2 == 1)
         b_transposes(2)
-        lora(2, False, (False, True))
-        lora(3, False, (False, True))
+        for i in range(4):
+            lora(1, i // 2, i % 2, i % 2 == 1)
         b_transposes(3)
-        lora(4, False, (False, True))
-        lora(5, False, (False, True))
-        hg = hgrp_pool.tile([P, 8 * T], BF16, name="hg", align_bytes=64)
-        h_transposes(0, 0, hg, True)
-        h_transposes(0, 1, hg, False)
-        h_quantise(0, 0, hg)
-        h_quantise(0, 1, hg)
-        nxt = w_tiles()
-        w_transposes(0, 0, nxt, (True, False))
-        w_transposes(0, 1, nxt, (True, False))
-        lora(6, False, (True, False))
-        w_quantise(nxt, 0)
+        for i in range(4):
+            lora(2, i // 2, i % 2, i % 2 == 1)
+        h_transposes(0, 0, True)
+        h_transposes(0, 1, False)
+        lora(3, 0, 0, True)
+        w_transposes(0, 0, True)
+        w_transposes(0, 1, False)
+        h_quantise(0)
+        lora(3, 0, 1, True)
+        w_transposes(1, 0, True)
+        w_transposes(1, 1, False)
+        w_quantise(0)
+        lora(3, 1, 0, True)
+        lora(3, 1, 1, True)
 
-        last = None
-        for j in range(NCHUNK):
-            cur = nxt
-            e, c = divmod(j, 2)
-            if j > 0:
-                final_add(j - 1, 0, last)
-            w_quantise(cur, 1)
-            if j > 0:
-                final_add(j - 1, 1, last)
-                nc.sync.dma_start(out=out_part(j - 1), in_=o_sb[j - 1][:])
-            accs = [product_tile("macc%d" % i2) for i2 in range(2)]
-            if j + 1 < NCHUNK:
-                nxt = w_tiles()
-                if e + 1 < E:
-                    if c == 0:
-                        hg = hgrp_pool.tile([P, 8 * T], BF16, name="hg", align_bytes=64)
-                    h_transposes(e + 1, c, hg, True)
-                w_transposes(j + 1, 0, nxt, (True, True))
-            else:
-                lora(7, True, (True, True))
-            mx_passes(j, 0, cur, accs)
-            if j + 1 < NCHUNK:
-                if e + 1 < E:
-                    h_quantise(e + 1, c, hg)
-                w_quantise(nxt, 0)
-                w_transposes(j + 1, 1, nxt, (True, True))
-            mx_passes(j, 1, cur, accs)
-            last = accs
-        for i2 in range(2):
-            final_add(NCHUNK - 1, i2, last)
-            nc.sync.dma_start(out=out_part(NCHUNK - 1)[:, i2, :], in_=o_sb[NCHUNK - 1][:, i2, :])
+        for u in range(NU):
+            e, s = divmod(u, UPE)
+            if e + 1 < E and s % 2 == 0:
+                h_transposes(e + 1, s // 2, True)
+            if u + 2 < NU:
+                w_transposes(u + 2, 0, True)
+                w_transposes(u + 2, 1, True)
+            if u > 0:
+                final_add(u - 1)
+                store(u - 1)
+            if u + 1 < NU:
+                w_quantise(u + 1)
+            mx_passes(u)
+            if e + 1 < E and s == 2:
+                h_quantise(e + 1)
+        final_add(NU - 1)
+        store(NU - 1)

@@ -169,6 +169,12 @@ def tile_loralinearexpertswrapper_pb_kernel(tc, h, low_d, W_d, B_d, out):
                 in_=grp[:],
             )
 
+        def quantise_pass(u, g):
+            grp, w_codes, w_scales = w_st[u]
+            nc.vector.quantize_mx(
+                out=w_codes[:, g, :].bitcast(FP8X4), scales=w_scales[:, g, :], in_=grp[:, 4 * UN * g : 4 * UN * g + 4 * UN]
+            )
+
         accs = {}
 
         def mx_passes(u):
@@ -193,6 +199,32 @@ def tile_loralinearexpertswrapper_pb_kernel(tc, h, low_d, W_d, B_d, out):
             dst = part.rearrange("p t (q i) -> p t q i", i=2)
             nc.vector.tensor_add(out=dst, in0=dst, in1=accs[u][:].rearrange("p (t i q) -> p t q i", t=2, i=2))
 
+        def last_unit_passes():
+            grp, w_codes, w_scales = w_st[NU - 1]
+            tiles = [product_tile("macc"), product_tile("macc")]
+            for g in range(2):
+                for i2 in range(2):
+                    nc.tensor.matmul_mx(
+                        out=tiles[i2][:, 0:UN],
+                        lhsT=h_codes[E - 1][:, g, P * i2 : P * i2 + P].bitcast(FP8X4),
+                        lhsT_scale=h_scales[E - 1][:, g, P * i2 : P * i2 + P],
+                        rhs=w_codes[:, g, :].bitcast(FP8X4),
+                        rhs_scale=w_scales[:, g, :],
+                        start=(g == 0),
+                        stop=(g == 1),
+                    )
+            return tiles
+
+        def last_unit_out(tiles):
+            rows = out[T * (E - 1) : T * E, UN * (UPE - 1) : UN * UPE].rearrange("(p i) n -> p i n", i=2)
+            for i2 in range(2):
+                part = o_last[:, UPE - 1, i2, :]
+                dst = part.rearrange("p (q i) -> p q i", i=2)
+                nc.vector.tensor_add(
+                    out=dst, in0=dst, in1=tiles[i2][:, 0:UN].rearrange("p (i q) -> p q i", i=2)
+                )
+                nc.sync.dma_start(out=rows[:, i2, :], in_=part)
+
         def store(u):
             e, s = divmod(u, UPE)
             rows = out[T * e : T * e + T, :].rearrange("(p i) n -> p i n", i=2)
@@ -201,7 +233,7 @@ def tile_loralinearexpertswrapper_pb_kernel(tc, h, low_d, W_d, B_d, out):
             elif s == UPE - 1:
                 nc.sync.dma_start(out=rows, in_=o_sb[e][:])
 
-        warm_up(6)
+        warm_up(4)
         b_transposes(0)
         b_transposes(1)
         for i in range(4):
@@ -230,15 +262,19 @@ def tile_loralinearexpertswrapper_pb_kernel(tc, h, low_d, W_d, B_d, out):
             if e + 1 < E and s % 2 == 0:
                 h_transposes(e + 1, s // 2, True)
             if u + 2 < NU:
-                w_transposes(u + 2, 0, True)
-                w_transposes(u + 2, 1, True)
+                w_transposes(u + 2, 0, u > 0)
+                w_transposes(u + 2, 1, u > 0)
+            if u + 2 == NU:
+                quantise_pass(NU - 1, 0)
             if u > 0:
                 final_add(u - 1)
                 store(u - 1)
-            if u + 1 < NU:
+            if u + 2 < NU:
                 w_quantise(u + 1)
-            mx_passes(u)
+            elif u + 2 == NU:
+                quantise_pass(NU - 1, 1)
+            if u + 1 < NU:
+                mx_passes(u)
             if e + 1 < E and s == 2:
                 h_quantise(e + 1)
-        final_add(NU - 1)
-        store(NU - 1)
+        last_unit_out(last_unit_passes())

@@ -36,33 +36,41 @@ def tile_loralinearexpertswrapper_pb_kernel(tc, h, low_d, W_d, B_d, out):
         ident_f = keep.tile([P, P], F32, name="ident_f")
         make_identity(nc, ident_f[:])
 
-        low_sb = []
-        b_sb = []
-        for e in range(E):
-            l_t = keep.tile([P, 2 * R], BF16, name="low_sb%d" % e)
-            nc.sync.dma_start(out=l_t[:], in_=low_d[e].rearrange("(p i) r -> p (i r)", i=2))
-            low_sb.append(l_t)
-            b_t = keep.tile([P, 8 * R], BF16, name="b_sb%d" % e)
-            nc.sync.dma_start(out=b_t[:], in_=B_d[e].rearrange("(p i) r -> p (i r)", i=8))
-            b_sb.append(b_t)
-        h_sb = []
-        w_sb = []
+        probe = keep.tile([P, 2], BF16, name="probe")
+        nc.scalar.copy(out=probe[:], in_=zero[:, 0:2])
+        low_head = [keep.tile([P, 2 * R], BF16, name="low_head%d" % e) for e in range(2)]
+        low_rest = keep.tile([P, E - 2, 2 * R], BF16, name="low_rest")
+        low_sb = [low_head[0][:], low_head[1][:]] + [low_rest[:, e, :] for e in range(E - 2)]
+        b_sb = [keep.tile([P, 8 * R], BF16, name="b_sb%d" % e) for e in range(E)]
+        h_sb = [keep.tile([P, 2 * D], BF16, name="h_sb%d" % e) for e in range(E)]
+        w_sb = [keep.tile([P, 2 * D], BF16, name="w_sb%d" % u) for u in range(NU)]
 
-        def load_h(e):
-            h_t = keep.tile([P, 2 * D], BF16, name="h_sb%d" % e)
-            nc.sync.dma_start(out=h_t[:], in_=h[e].rearrange("(p i) k -> p (i k)", i=2))
-            h_sb.append(h_t)
+        def load_b(e):
+            nc.sync.dma_start(out=b_sb[e][:], in_=B_d[e].rearrange("(p i) r -> p (i r)", i=8))
 
-        load_h(0)
-        for u in range(NU):
+        def load_h(queue, e):
+            queue.dma_start(out=h_sb[e][:], in_=h[e].rearrange("(p i) k -> p (i k)", i=2))
+
+        def load_w(queue, u):
             e, s = divmod(u, UPE)
-            w_t = keep.tile([P, 2 * D], BF16, name="w_sb%d" % u)
-            nc.sync.dma_start(
-                out=w_t[:], in_=W_d[e, UN * s : UN * s + UN, :].rearrange("(p i) k -> p (i k)", i=2)
+            queue.dma_start(
+                out=w_sb[u][:], in_=W_d[e, UN * s : UN * s + UN, :].rearrange("(p i) k -> p (i k)", i=2)
             )
-            w_sb.append(w_t)
-            if s == 1 and e + 1 < E:
-                load_h(e + 1)
+
+        for e in range(2):
+            nc.sync.dma_start(out=low_sb[e], in_=low_d[e].rearrange("(p i) r -> p (i r)", i=2))
+            load_b(e)
+        load_h(nc.scalar, 0)
+        load_w(nc.scalar, 0)
+        load_w(nc.scalar, 1)
+        nc.sync.dma_start(out=low_rest[:], in_=low_d[2:E].rearrange("e (p i) r -> p e (i r)", i=2))
+        for e in range(2, E):
+            load_b(e)
+        load_h(nc.sync, 1)
+        for u in range(2, NU):
+            load_w(nc.sync, u)
+            if u % UPE == 1 and u // UPE + 1 < E:
+                load_h(nc.sync, u // UPE + 1)
 
         lora_t = [keep.tile([P, 10, P], BF16, name="lora_t%d" % e) for e in range(E)]
         o_sb = [keep.tile([P, 2, H], F32, name="o_sb%d" % e) for e in range(E - 1)]

@@ -16,7 +16,8 @@ FLOPS = 2 * E * T * H * (D + R)
 UN = 256
 UPE = H // UN
 NU = E * UPE
-T_BANKS = 4
+HEAD_T, MAIN_T = (0, 1, 2, 3), (2, 3, 0, 1, 4)
+HEAD_P, MAIN_P = (4, 5, 6, 7), (5, 6, 7)
 
 
 def tile_loralinearexpertswrapper_pb_kernel(tc, h, low_d, W_d, B_d, out):
@@ -83,12 +84,14 @@ def tile_loralinearexpertswrapper_pb_kernel(tc, h, low_d, W_d, B_d, out):
         def transpose_tile(shape, dtype, name):
             n = taken[0]
             taken[0] = n + 1
-            return psum.tile(shape, dtype, name=name, tag="bank%d" % (n % T_BANKS))
+            bank = HEAD_T[n % 4] if n < 14 else MAIN_T[(n - 14) % len(MAIN_T)]
+            return psum.tile(shape, dtype, name=name, tag="bank%d" % bank)
 
         def product_tile(name):
             n = taken[1]
             taken[1] = n + 1
-            return psum.tile([P, 512], F32, name=name, tag="bank%d" % (T_BANKS + n % (8 - T_BANKS)))
+            bank = HEAD_P[n % 4] if n < 17 else MAIN_P[(n - 17) % len(MAIN_P)]
+            return psum.tile([P, 512], F32, name=name, tag="bank%d" % bank)
 
         def copy_out(on_scalar, dst, src):
             if on_scalar:
@@ -241,7 +244,7 @@ def tile_loralinearexpertswrapper_pb_kernel(tc, h, low_d, W_d, B_d, out):
             elif s == UPE - 1:
                 nc.sync.dma_start(out=rows, in_=o_sb[e][:])
 
-        warm_up(4)
+        warm_up(3)
         b_transposes(0)
         b_transposes(1)
         for i in range(4):

@@ -47,7 +47,9 @@ def tile_loralinearexpertswrapper_pb_kernel(tc, h, low_d, W_d, B_d, out):
         w_sb = [keep.tile([P, 2 * D], BF16, name="w_sb%d" % u) for u in range(NU)]
 
         def load_b(e):
-            nc.sync.dma_start(out=b_sb[e][:], in_=B_d[e].rearrange("(p i) r -> p (i r)", i=8))
+            rows = B_d[e].rearrange("(p i) r -> p (i r)", i=8)
+            for part in (slice(0, 4 * R), slice(4 * R, 8 * R)) if e == 0 else (slice(0, 8 * R),):
+                nc.sync.dma_start(out=b_sb[e][:, part], in_=rows[:, part])
 
         def load_h(queue, e):
             queue.dma_start(out=h_sb[e][:], in_=h[e].rearrange("(p i) k -> p (i k)", i=2))
@@ -246,9 +248,11 @@ def tile_loralinearexpertswrapper_pb_kernel(tc, h, low_d, W_d, B_d, out):
 
         warm_up(3)
         b_transposes(0)
+        for i in range(2):
+            lora(0, 0, i, i == 1)
         b_transposes(1)
-        for i in range(4):
-            lora(0, i // 2, i % 2, i % 2 == 1)
+        for i in range(2):
+            lora(0, 1, i, i == 1)
         b_transposes(2)
         for i in range(4):
             lora(1, i // 2, i % 2, i % 2 == 1)

from contextlib import ExitStack

import concourse.mybir as mybir
from concourse.masks import make_identity

F32 = mybir.dt.float32
BF16 = mybir.dt.bfloat16
U32 = mybir.dt.uint32
U8 = mybir.dt.uint8
FP8X4 = mybir.dt.float8_e4m3fn_x4

P = 128
E, T, H, D, R = 4, 256, 1024, 1024, 128
SCALE = 2.0
FLOPS = 2 * E * T * H * (D + R)
UN = 256
UPE = H // UN
NU = E * UPE
HEAD_T, MAIN_T = (0, 1, 2, 3), (2, 3, 0, 1, 4)
HEAD_P, MAIN_P = (4, 5, 6, 7), (5, 6, 7)


def tile_loralinearexpertswrapper_pb_kernel(tc, h, low_d, W_d, B_d, out):
    nc = tc.nc
    with ExitStack() as ctx:
        keep = ctx.enter_context(tc.tile_pool(name="keep", bufs=1))
        grp_pool = ctx.enter_context(tc.tile_pool(name="grp", bufs=4))
        hgrp_pool = ctx.enter_context(tc.tile_pool(name="hgrp", bufs=2))
        wq_pool = ctx.enter_context(tc.tile_pool(name="wq", bufs=4))
        psum = ctx.enter_context(tc.psum_pool(name="psum", bufs=1))
        ctx.enter_context(tc.manual_schedule())

        zero = keep.tile([P, 512], BF16, name="zero")
        nc.vector.memset(zero[:], 0.0)
        ident_bf = keep.tile([P, P], BF16, name="ident_bf")
        make_identity(nc, ident_bf[:])
        ident_f = keep.tile([P, P], F32, name="ident_f")
        make_identity(nc, ident_f[:])

        probe = keep.tile([P, 2], BF16, name="probe")
        nc.scalar.copy(out=probe[:], in_=zero[:, 0:2])
        low_head = [keep.tile([P, 2 * R], BF16, name="low_head%d" % e) for e in range(2)]
        low_rest = keep.tile([P, E - 2, 2 * R], BF16, name="low_rest")
        low_sb = [low_head[0][:], low_head[1][:]] + [low_rest[:, e, :] for e in range(E - 2)]
        b_sb = [keep.tile([P, 8 * R], BF16, name="b_sb%d" % e) for e in range(E)]
        h_sb = [keep.tile([P, 2 * D], BF16, name="h_sb%d" % e) for e in range(E)]
        w_sb = [keep.tile([P, 2 * D], BF16, name="w_sb%d" % u) for u in range(NU)]

        def load_b(e):
            rows = B_d[e].rearrange("(p i) r -> p (i r)", i=8)
            for part in (slice(0, 4 * R), slice(4 * R, 8 * R)) if e == 0 else (slice(0, 8 * R),):
                nc.sync.dma_start(out=b_sb[e][:, part], in_=rows[:, part])

        def load_h(queue, e):
            queue.dma_start(out=h_sb[e][:], in_=h[e].rearrange("(p i) k -> p (i k)", i=2))

        def load_w(queue, u):
            e, s = divmod(u, UPE)
            queue.dma_start(
                out=w_sb[u][:], in_=W_d[e, UN * s : UN * s + UN, :].rearrange("(p i) k -> p (i k)", i=2)
            )

        for e in range(2):
            nc.sync.dma_start(out=low_sb[e], in_=low_d[e].rearrange("(p i) r -> p (i r)", i=2))
            load_b(e)
        load_h(nc.scalar, 0)
        load_w(nc.scalar, 0)
        load_w(nc.scalar, 1)
        nc.sync.dma_start(out=low_rest[:], in_=low_d[2:E].rearrange("e (p i) r -> p e (i r)", i=2))
        for e in range(2, E):
            load_b(e)
        load_h(nc.sync, 1)
        for u in range(2, NU):
            load_w(nc.sync, u)
            if u % UPE == 1 and u // UPE + 1 < E:
                load_h(nc.sync, u // UPE + 1)

        lora_t = [keep.tile([P, 10, P], BF16, name="lora_t%d" % e) for e in range(E)]
        o_sb = [keep.tile([P, 2, H], F32, name="o_sb%d" % e) for e in range(E - 1)]
        o_last = keep.tile([P, UPE, 2, UN], F32, name="o_last")
        h_codes = [keep.tile([P, 2, T], U32, name="h_codes%d" % e, align_bytes=64) for e in range(E)]
        h_scales = [keep.tile([P, 2, T], U8, name="h_scales%d" % e, align_bytes=64) for e in range(E)]

        taken = [0, 0]

        def transpose_tile(shape, dtype, name):
            n = taken[0]
            taken[0] = n + 1
            bank = HEAD_T[n % 4] if n < 14 else MAIN_T[(n - 14) % len(MAIN_T)]
            return psum.tile(shape, dtype, name=name, tag="bank%d" % bank)

        def product_tile(name):
            n = taken[1]
            taken[1] = n + 1
            bank = HEAD_P[n % 4] if n < 17 else MAIN_P[(n - 17) % len(MAIN_P)]
            return psum.tile([P, 512], F32, name=name, tag="bank%d" % bank)

        def copy_out(on_scalar, dst, src):
            if on_scalar:
                nc.scalar.copy(out=dst, in_=src)
            else:
                nc.vector.tensor_copy(out=dst, in_=src)

        def warm_up(n):
            dummy = product_tile("dummy")
            for d in range(n):
                nc.tensor.matmul(out=dummy[:], lhsT=zero[:, 0:P], rhs=zero[:], start=True, stop=True)

        def b_transposes(e):
            xa = transpose_tile([P, 6, P], BF16, "xa")
            for i in range(2):
                nc.tensor.transpose(xa[:, i, :], low_sb[e][:, P * i : P * i + P], ident_bf[:])
            for i in range(4):
                nc.tensor.transpose(xa[:, 2 + i, :], b_sb[e][:, P * i : P * i + P], ident_bf[:])
            copy_out(False, lora_t[e][:, 0:6, :], xa[:])
            xb = transpose_tile([P, 4, P], BF16, "xb")
            for i in range(4):
                nc.tensor.transpose(xb[:, i, :], b_sb[e][:, P * (4 + i) : P * (4 + i) + P], ident_bf[:])
            copy_out(True, lora_t[e][:, 6:10, :], xb[:])

        def lora(e, c, i2, on_scalar):
            acc = product_tile("acc")
            nc.tensor.matmul(
                out=acc[:],
                lhsT=lora_t[e][:, i2, :],
                rhs=lora_t[e][:, 2 + 4 * c : 6 + 4 * c, :].rearrange("p i q -> p (i q)"),
                start=True,
                stop=True,
            )
            if e < E - 1:
                dst = o_sb[e][:, i2, :].rearrange("p (q i) -> p q i", i=8)[:, :, 4 * c : 4 * c + 4]
                src = acc[:].rearrange("p (i q) -> p q i", i=4)
            else:
                dst = o_last[:, :, i2, :].rearrange("p s (q i) -> p s q i", i=8)[:, :, :, 4 * c : 4 * c + 4]
                src = acc[:].rearrange("p (i s q) -> p s q i", i=4, s=UPE)
            if on_scalar:
                nc.scalar.mul(out=dst, in_=src, mul=SCALE)
            else:
                nc.vector.tensor_scalar_mul(out=dst, in0=src, scalar1=SCALE)

        def word_transposes(src_f32, g, dst_f32, on_scalar):
            xt = transpose_tile([P, 2, 256], F32, "xt")
            for u in range(2):
                for i in range(2):
                    col = 512 * i + 256 * g + P * u
                    nc.tensor.transpose(xt[:, u, P * i : P * i + P], src_f32[:, col : col + P], ident_f[:])
            copy_out(on_scalar, dst_f32.rearrange("p (n u) -> p n u", u=2), xt[:].rearrange("p u n -> p n u"))

        h_grp = {}

        def h_transposes(e, g, on_scalar):
            if g == 0:
                h_grp[e] = hgrp_pool.tile([P, 8 * T], BF16, name="hg", align_bytes=64)
            word_transposes(
                h_sb[e][:].bitcast(F32), g, h_grp[e][:].bitcast(F32)[:, 512 * g : 512 * g + 512], on_scalar
            )

        def h_quantise(e):
            nc.vector.quantize_mx(
                out=h_codes[e][:].rearrange("p g n -> p (g n)").bitcast(FP8X4),
                scales=h_scales[e][:].rearrange("p g n -> p (g n)"),
                in_=h_grp[e][:],
            )

        w_st = {}

        def w_transposes(u, g, on_scalar):
            if g == 0:
                grp = grp_pool.tile([P, 2048], BF16, name="grp", align_bytes=64)
                w_codes = wq_pool.tile([P, 2, UN], U32, name="w_codes", align_bytes=64)
                w_scales = wq_pool.tile([P, 2, UN], U8, name="w_scales", align_bytes=64)
                w_st[u] = (grp, w_codes, w_scales)
            word_transposes(
                w_sb[u][:].bitcast(F32), g, w_st[u][0][:].bitcast(F32)[:, 512 * g : 512 * g + 512], on_scalar
            )

        def w_quantise(u):
            grp, w_codes, w_scales = w_st[u]
            nc.vector.quantize_mx(
                out=w_codes[:].rearrange("p g n -> p (g n)").bitcast(FP8X4),
                scales=w_scales[:].rearrange("p g n -> p (g n)"),
                in_=grp[:],
            )

        def quantise_pass(u, g):
            grp, w_codes, w_scales = w_st[u]
            nc.vector.quantize_mx(
                out=w_codes[:, g, :].bitcast(FP8X4), scales=w_scales[:, g, :], in_=grp[:, 4 * UN * g : 4 * UN * g + 4 * UN]
            )

        accs = {}

        def mx_passes(u):
            e = u // UPE
            grp, w_codes, w_scales = w_st[u]
            accs[u] = product_tile("macc")
            for i2 in range(2):
                for g in range(2):
                    nc.tensor.matmul_mx(
                        out=accs[u][:, UN * i2 : UN * i2 + UN],
                        lhsT=h_codes[e][:, g, P * i2 : P * i2 + P].bitcast(FP8X4),
                        lhsT_scale=h_scales[e][:, g, P * i2 : P * i2 + P],
                        rhs=w_codes[:, g, :].bitcast(FP8X4),
                        rhs_scale=w_scales[:, g, :],
                        start=(g == 0),
                        stop=(g == 1),
                    )

        def final_add(u):
            e, s = divmod(u, UPE)
            part = o_sb[e][:, :, UN * s : UN * s + UN] if e < E - 1 else o_last[:, s, :, :]
            dst = part.rearrange("p t (q i) -> p t q i", i=2)
            nc.vector.tensor_add(out=dst, in0=dst, in1=accs[u][:].rearrange("p (t i q) -> p t q i", t=2, i=2))

        def last_unit_passes():
            grp, w_codes, w_scales = w_st[NU - 1]
            tiles = [product_tile("macc"), product_tile("macc")]
            for g in range(2):
                for i2 in range(2):
                    nc.tensor.matmul_mx(
                        out=tiles[i2][:, 0:UN],
                        lhsT=h_codes[E - 1][:, g, P * i2 : P * i2 + P].bitcast(FP8X4),
                        lhsT_scale=h_scales[E - 1][:, g, P * i2 : P * i2 + P],
                        rhs=w_codes[:, g, :].bitcast(FP8X4),
                        rhs_scale=w_scales[:, g, :],
                        start=(g == 0),
                        stop=(g == 1),
                    )
            return tiles

        def last_unit_out(tiles):
            rows = out[T * (E - 1) : T * E, UN * (UPE - 1) : UN * UPE].rearrange("(p i) n -> p i n", i=2)
            for i2 in range(2):
                part = o_last[:, UPE - 1, i2, :]
                dst = part.rearrange("p (q i) -> p q i", i=2)
                nc.vector.tensor_add(
                    out=dst, in0=dst, in1=tiles[i2][:, 0:UN].rearrange("p (i q) -> p q i", i=2)
                )
                nc.sync.dma_start(out=rows[:, i2, :], in_=part)

        def store(u):
            e, s = divmod(u, UPE)
            rows = out[T * e : T * e + T, :].rearrange("(p i) n -> p i n", i=2)
            if e == E - 1:
                nc.sync.dma_start(out=rows[:, :, UN * s : UN * s + UN], in_=o_last[:, s, :, :])
            elif s == UPE - 1:
                nc.sync.dma_start(out=rows, in_=o_sb[e][:])

        warm_up(3)
        b_transposes(0)
        for i in range(2):
            lora(0, 0, i, i == 1)
        b_transposes(1)
        for i in range(2):
            lora(0, 1, i, i == 1)
        b_transposes(2)
        for i in range(4):
            lora(1, i // 2, i % 2, i % 2 == 1)
        b_transposes(3)
        for i in range(4):
            lora(2, i // 2, i % 2, i % 2 == 1)
        h_transposes(0, 0, True)
        h_transposes(0, 1, False)
        lora(3, 0, 0, True)
        w_transposes(0, 0, True)
        w_transposes(0, 1, False)
        h_quantise(0)
        lora(3, 0, 1, True)
        w_transposes(1, 0, True)
        w_transposes(1, 1, False)
        w_quantise(0)
        lora(3, 1, 0, True)
        lora(3, 1, 1, True)

        for u in range(NU):
            e, s = divmod(u, UPE)
            if e + 1 < E and s % 2 == 0:
                h_transposes(e + 1, s // 2, True)
            if u + 2 < NU:
                w_transposes(u + 2, 0, u > 0)
                w_transposes(u + 2, 1, u > 0)
            if u + 2 == NU:
                quantise_pass(NU - 1, 0)
            if u > 0:
                final_add(u - 1)
                store(u - 1)
            if u + 2 < NU:
                w_quantise(u + 1)
            elif u + 2 == NU:
                quantise_pass(NU - 1, 1)
            if u + 1 < NU:
                mx_passes(u)
            if e + 1 < E and s == 2:
                h_quantise(e + 1)
        last_unit_out(last_unit_passes())
